import numpy as np
import ml_dtypes


def mxq(x, axis, fmt="e4m3"):
    dtype, down = {"e4m3": (ml_dtypes.float8_e4m3fn, 7), "e5m2": (ml_dtypes.float8_e5m2, 14)}[fmt]
    v = np.moveaxis(np.asarray(x, np.float32).astype(ml_dtypes.bfloat16).astype(np.float64), axis, -1)
    blocks = v.reshape(v.shape[:-1] + (-1, 32))
    amax = np.abs(blocks).max(-1, keepdims=True)
    byte = np.maximum(np.where(amax > 0, np.frexp(amax)[1] - 1 + 127, 0) - down, 1)
    scale = np.exp2(byte - 127.0)
    codes = (blocks / scale).astype(np.float32).astype(dtype).astype(np.float64)
    return np.moveaxis((codes * scale).reshape(v.shape), -1, axis)


WIDE = False


def mx_kscale(k):
    if not WIDE:
        return np.ones(k)
    levels = np.array([10, -10, 5, -5, 0])
    a = np.random.permutation(np.resize(levels, k // 512 * 4)).reshape(k // 512, 4)
    idx = np.arange(k)
    return np.exp2(a[idx // 512, idx % 128 // 32])


BF16 = ml_dtypes.bfloat16


def bf(x):
    return np.asarray(x, np.float32).astype(BF16)


def f64(x):
    return np.asarray(x).astype(np.float64)


B, S, D, H, NOPE, ROPE, VD, KV_RANK, Q_RANK = 4, 2048, 1024, 2, 64, 64, 128, 512, 512
EPS = 1e-6
THETA = 10000.0
LAT = 0.005
HALF = ROPE // 2
QK = NOPE + ROPE


def rmsnorm(v, g):
    return v * (1.0 / np.sqrt(np.mean(v * v, axis=-1, keepdims=True) + EPS)) * g


def rope(v):
    inv = 1.0 / THETA ** (np.arange(HALF) / HALF)
    ang = np.arange(S)[:, None] * inv[None, :]
    cos = np.cos(ang)[None, :, None, :]
    sin = np.sin(ang)[None, :, None, :]
    v1, v2 = v[..., :HALF], v[..., HALF:]
    return np.concatenate([v1 * cos - v2 * sin, v2 * cos + v1 * sin], axis=-1)


def setup_inputs():
    s, t = mx_kscale(D), mx_kscale(Q_RANK)
    return {"x": bf(np.random.standard_normal((B, S, D)) * s),
            "w_dq": bf(np.random.standard_normal((D, Q_RANK)) * LAT / np.sqrt(D) / s[:, None]),
            "q_a_norm": bf((1.0 + 0.1 * np.random.standard_normal(Q_RANK)) * t),
            "w_uq": bf(np.random.standard_normal((Q_RANK, H * QK)) / np.sqrt(Q_RANK) / t[:, None])}


def reference(x, w_dq, q_a_norm, w_uq):
    c_q = mxq(f64(x), 2, "e4m3") @ mxq(f64(w_dq), 0, "e4m3")
    h = rmsnorm(c_q, f64(q_a_norm))
    q = (mxq(h, 2, "e4m3") @ mxq(f64(w_uq), 0, "e4m3")).reshape(B, S, H, QK)
    q_nope, q_pe = q[..., :NOPE], q[..., NOPE:]
    return np.concatenate([q_nope, rope(q_pe)], axis=-1)

@@ -1,0 +1,261 @@
+from contextlib import ExitStack
+import math
+
+import concourse.mybir as mybir
+from concourse.masks import make_identity
+
+F32 = mybir.dt.float32
+BF16 = mybir.dt.bfloat16
+I32 = mybir.dt.int32
+U32 = mybir.dt.uint32
+U8 = mybir.dt.uint8
+FP8X4 = mybir.dt.float8_e4m3fn_x4
+ALU = mybir.AluOpType
+ACT = mybir.ActivationFunctionType
+
+P = 128
+B, S, D, H, NOPE, ROPE, Q_RANK = 4, 2048, 1024, 2, 64, 64, 512
+QK = NOPE + ROPE
+HALF = ROPE // 2
+NOUT = H * QK
+EPS = 1e-6
+THETA = 10000.0
+TPB = S // P
+UNIT = 2
+UPB = TPB // UNIT
+UNITS = B * UPB
+AHEAD = 5
+MANUAL = True
+VEC_COPY = (1, 3)
+VEC_MOD = 5
+
+FLOPS = 2 * B * S * (D * Q_RANK + Q_RANK * NOUT)
+
+GRID = 2 ** 15
+
+
+def tile_multiheadlatentattention_pa_t_kernel(tc, x, w_dq, q_a_norm, w_uq, out):
+    nc = tc.nc
+    xv = x.rearrange("b (p t) k -> b p t k", t=TPB)
+    ov = out.rearrange("b (p t) h f -> b p t (h f)", t=TPB)
+
+    with ExitStack() as ctx:
+        const = ctx.enter_context(tc.tile_pool(name="const", bufs=1))
+        setup = ctx.enter_context(tc.tile_pool(name="setup", bufs=1))
+        xpool = ctx.enter_context(tc.tile_pool(name="xpool", bufs=AHEAD + 1))
+        work = ctx.enter_context(tc.tile_pool(name="work", bufs=3))
+        small = ctx.enter_context(tc.tile_pool(name="small", bufs=4))
+        psum = ctx.enter_context(tc.psum_pool(name="psum", bufs=1))
+        if MANUAL:
+            ctx.enter_context(tc.manual_schedule())
+
+        st = {}
+
+        def load(u):
+            x_sb = xpool.tile([P, UNIT, D], BF16, name="x_sb")
+            b, t0 = u // UPB, (u % UPB) * UNIT
+            nc.sync.dma_start(out=x_sb[:], in_=xv[b, :, t0:t0 + UNIT, :])
+            st["x", u] = x_sb
+
+        w_raw = setup.tile([P, 4, 2 * Q_RANK], BF16)
+        w_view = w_dq.rearrange("(a p e) c -> p a (e c)", a=4, p=P, e=2)
+        nc.sync.dma_start(out=w_raw[:, 0:2, :], in_=w_view[:, 0:2, :])
+        load(0)
+        nc.sync.dma_start(out=w_raw[:, 2:4, :], in_=w_view[:, 2:4, :])
+        for u in range(1, AHEAD):
+            load(u)
+        u_raw = setup.tile([P, 4, NOUT], BF16)
+        nc.scalar.dma_start(out=u_raw[:], in_=w_uq.rearrange("(j p) n -> p j n", p=P))
+        g_b = const.tile([P, Q_RANK], BF16)
+        nc.gpsimd.dma_start(out=g_b[:], in_=q_a_norm.partition_broadcast(P))
+
+        ident_f = const.tile([P, P], F32)
+        make_identity(nc, ident_f[:])
+        pos_i = setup.tile([P, TPB], I32)
+        nc.gpsimd.iota(pos_i[:], pattern=[[1, TPB]], base=0, channel_multiplier=TPB)
+        ident_b = const.tile([P, P], BF16)
+        make_identity(nc, ident_b[:])
+
+        pos_f = setup.tile([P, TPB], F32)
+        nc.vector.tensor_copy(out=pos_f[:], in_=pos_i[:])
+        turn_i = setup.tile([P, 2, TPB, HALF], I32)
+        turn_lo = setup.tile([P, TPB, HALF], F32)
+        for i in range(HALF):
+            freq = 1.0 / THETA ** (i / HALF) / (2.0 * math.pi)
+            f_hi = math.floor(freq * GRID)
+            f_lo = freq - f_hi / GRID
+            nc.vector.tensor_scalar(out=turn_i[:, 0, :, i], in0=pos_f[:], scalar1=float(f_hi),
+                                    scalar2=float(GRID // 2), op0=ALU.mult, op1=ALU.add)
+            nc.vector.tensor_scalar(out=turn_lo[:, :, i], in0=pos_f[:], scalar1=f_lo,
+                                    scalar2=None, op0=ALU.mult)
+        frac = setup.tile([P, 2, TPB * HALF], F32)
+        negf = setup.tile([P, 2, TPB, HALF], F32)
+        cos_t = const.tile([P, TPB, HALF], F32)
+        sin_t = const.tile([P, TPB, 2, HALF], F32)
+
+        def tables_vector():
+            nc.vector.tensor_scalar(out=turn_i[:, 1], in0=turn_i[:, 0], scalar1=float(GRID // 4),
+                                    scalar2=None, op0=ALU.add)
+            nc.vector.tensor_scalar(out=turn_i[:], in0=turn_i[:], scalar1=GRID - 1,
+                                    scalar2=None, op0=ALU.bitwise_and)
+            nc.vector.scalar_tensor_tensor(
+                out=frac[:], in0=turn_i[:].rearrange("p a t i -> p a (t i)"), scalar=1.0 / GRID,
+                in1=turn_lo[:].rearrange("p t i -> p (t i)").unsqueeze(1).to_broadcast([P, 2, TPB * HALF]),
+                op0=ALU.mult, op1=ALU.add)
+            nc.vector.scalar_tensor_tensor(
+                out=negf[:].rearrange("p a t i -> p a (t i)"), in0=frac[:], scalar=1.0, in1=frac[:],
+                op0=ALU.is_ge, op1=ALU.subtract)
+
+        def tables_scalar():
+            nc.scalar.activation(out=cos_t[:], in_=negf[:, 1], func=ACT.Sin, scale=-2.0 * math.pi, bias=-math.pi)
+            nc.scalar.activation(out=sin_t[:, :, 0, :], in_=negf[:, 0], func=ACT.Sin,
+                                 scale=-2.0 * math.pi, bias=-math.pi)
+            nc.scalar.activation(out=sin_t[:, :, 1, :], in_=negf[:, 0], func=ACT.Sin,
+                                 scale=2.0 * math.pi, bias=math.pi)
+
+        wdq_c = const.tile([P, 2, Q_RANK], U32, align_bytes=64)
+        wdq_s = const.tile([P, 2, Q_RANK], U8, align_bytes=64)
+        w_grps = []
+        for g in range(2):
+            w_grp = setup.tile([P, Q_RANK, 4], BF16, align_bytes=64, name="w_grp%d" % g)
+            w_src = w_raw[:, 2 * g:2 * g + 2, :].rearrange("p u (e c) -> p (u e) c", e=2)
+            nc.vector.tensor_copy(out=w_grp[:].rearrange("p (c i) t -> p c t i", i=4),
+                                  in_=w_src.rearrange("p t (c i) -> p c t i", i=4))
+            w_grps.append(w_grp)
+        for g in range(2):
+            nc.vector.quantize_mx(out=wdq_c[:, g, :].bitcast(FP8X4), scales=wdq_s[:, g, :],
+                                  in_=w_grps[g][:].rearrange("p c t -> p (c t)"))
+        wuq_c = const.tile([P, NOUT], U32, align_bytes=64)
+        wuq_s = const.tile([P, NOUT], U8, align_bytes=64)
+        u_grp = setup.tile([P, 2, H, NOPE, 4], BF16, align_bytes=64)
+
+        def weights_up():
+            u_src = u_raw[:].rearrange("p j (h r f) -> p r h f j", h=H, r=2)
+            for r in range(2):
+                nc.vector.tensor_copy(out=u_grp[:, r], in_=u_src[:, r])
+            nc.vector.quantize_mx(out=wuq_c[:].bitcast(FP8X4), scales=wuq_s[:],
+                                  in_=u_grp[:].rearrange("p r h f j -> p (r h f j)"))
+
+        def t_x(u):
+            x_sb = st["x", u]
+            xg = work.tile([P, UNIT, 2, P, 4], BF16, align_bytes=64, name="xg")
+            for i in range(UNIT):
+                xt = psum.tile([P, 4, P], F32, name="xt", bufs=2)
+                words = x_sb[:, i, :].bitcast(F32)
+                for a in range(4):
+                    nc.tensor.transpose(xt[:, a, :], words[:, a * P:(a + 1) * P], ident_f[:])
+                planes = xt[:].rearrange("p (g u) w -> p g w u", u=2)
+                if i == 1 and u % VEC_MOD in VEC_COPY:
+                    nc.vector.tensor_copy(out=xg[:, i].bitcast(F32), in_=planes)
+                else:
+                    nc.scalar.copy(out=xg[:, i].bitcast(F32), in_=planes)
+            st["xg", u] = xg
+
+        def q_x(u):
+            xg = st["xg", u]
+            xc = work.tile([P, UNIT * 2 * P], U32, align_bytes=64, name="xc")
+            xs = work.tile([P, UNIT * 2 * P], U8, align_bytes=64, name="xs")
+            nc.vector.quantize_mx(out=xc[:].bitcast(FP8X4), scales=xs[:],
+                                  in_=xg[:].rearrange("p i g w t -> p (i g w t)"))
+            st["xc", u] = (xc, xs)
+
+        def mx1(u):
+            xc, xs = st["xc", u]
+            ss = small.tile([P, UNIT], F32, name="ss")
+            cs = []
+            for i in range(UNIT):
+                c_ps = psum.tile([P, Q_RANK], F32, name="c_ps", bufs=4)
+                for g in range(2):
+                    cols = slice((2 * i + g) * P, (2 * i + g + 1) * P)
+                    nc.tensor.matmul_mx(out=c_ps[:], lhsT=xc[:, cols].bitcast(FP8X4), lhsT_scale=xs[:, cols],
+                                        rhs=wdq_c[:, g, :].bitcast(FP8X4), rhs_scale=wdq_s[:, g, :],
+                                        start=(g == 0), stop=(g == 1))
+                cs.append(c_ps)
+            for i in range(UNIT):
+                junk = work.tile([P, Q_RANK], BF16, name="junk")
+                nc.scalar.activation(out=junk[:], in_=cs[i][:], func=ACT.Square, accum_out=ss[:, i:i + 1])
+            rms = small.tile([P, UNIT], F32, name="rms")
+            nc.scalar.activation(out=rms[:], in_=ss[:], func=ACT.Sqrt, scale=1.0 / Q_RANK, bias=EPS)
+            st["c", u] = (cs, rms)
+
+        def norm(u):
+            cs, rms = st["c", u]
+            rstd = small.tile([P, UNIT], F32, name="rstd")
+            nc.vector.reciprocal(rstd[:], rms[:])
+            h_sb = work.tile([P, UNIT, Q_RANK], BF16, name="h_sb")
+            for i in range(UNIT):
+                nc.vector.scalar_tensor_tensor(out=h_sb[:, i, :], in0=cs[i][:], scalar=rstd[:, i:i + 1],
+                                               in1=g_b[:], op0=ALU.mult, op1=ALU.mult)
+            st["h", u] = h_sb
+
+        def t_h(u):
+            h_sb = st["h", u]
+            ht = psum.tile([P, UNIT, 4, P], BF16, name="ht", bufs=1)
+            for i in range(UNIT):
+                for j in range(4):
+                    nc.tensor.transpose(ht[:, i, j, :], h_sb[:, i, j * P:(j + 1) * P], ident_b[:])
+            hg = work.tile([P, UNIT, P, 4], BF16, align_bytes=64, name="hg")
+            nc.scalar.copy(out=hg[:], in_=ht[:].rearrange("p i j w -> p i w j"))
+            st["hg", u] = hg
+
+        def q_h(u):
+            hg = st["hg", u]
+            hc = work.tile([P, UNIT * P], U32, align_bytes=64, name="hc")
+            hs = work.tile([P, UNIT * P], U8, align_bytes=64, name="hs")
+            nc.vector.quantize_mx(out=hc[:].bitcast(FP8X4), scales=hs[:],
+                                  in_=hg[:].rearrange("p i w j -> p (i w j)"))
+            st["hc", u] = (hc, hs)
+
+        def mx2(u):
+            hc, hs = st["hc", u]
+            q_ps = psum.tile([P, UNIT, NOUT], F32, name="q_ps", bufs=1)
+            for i in range(UNIT):
+                cols = slice(i * P, (i + 1) * P)
+                nc.tensor.matmul_mx(out=q_ps[:, i, :], lhsT=hc[:, cols].bitcast(FP8X4), lhsT_scale=hs[:, cols],
+                                    rhs=wuq_c[:].bitcast(FP8X4), rhs_scale=wuq_s[:], start=True, stop=True)
+            st["q", u] = q_ps
+
+        def rope(u):
+            q_ps = st["q", u]
+            b, t0 = u // UPB, (u % UPB) * UNIT
+            o_sb = work.tile([P, UNIT, H, QK], F32, name="o_sb", bufs=4)
+            by_cos = work.tile([P, UNIT, H, 2, HALF], F32, name="by_cos")
+            by_sin = work.tile([P, UNIT, H, 2, HALF], F32, name="by_sin")
+            nc.vector.tensor_tensor(
+                out=by_cos[:].rearrange("p i h r f -> p i (h r) f"),
+                in0=q_ps[:, :, H * NOPE:].rearrange("p i (a f) -> p i a f", f=HALF),
+                in1=cos_t[:, t0:t0 + UNIT, :].unsqueeze(2).to_broadcast([P, UNIT, 2 * H, HALF]),
+                op=ALU.mult)
+            nc.vector.tensor_tensor(
+                out=by_sin[:].rearrange("p i h r f -> p i h (r f)"),
+                in0=q_ps[:, :, H * NOPE:].rearrange("p i (h f) -> p i h f", h=H),
+                in1=sin_t[:, t0:t0 + UNIT].rearrange("p i r f -> p i (r f)").unsqueeze(2).to_broadcast(
+                    [P, UNIT, H, ROPE]),
+                op=ALU.mult)
+            nc.vector.tensor_copy(out=o_sb[:, :, :, 0:NOPE],
+                                  in_=q_ps[:, :, 0:H * NOPE].rearrange("p i (h f) -> p i h f", h=H))
+            for r in range(2):
+                nc.gpsimd.tensor_tensor(out=o_sb[:, :, :, NOPE + r * HALF:NOPE + (r + 1) * HALF],
+                                        in0=by_cos[:, :, :, r, :], in1=by_sin[:, :, :, 1 - r, :], op=ALU.add)
+            nc.sync.dma_start(out=ov[b, :, t0:t0 + UNIT, :], in_=o_sb[:].rearrange("p i h f -> p i (h f)"))
+
+        def on(fn, u):
+            if 0 <= u < UNITS:
+                fn(u)
+
+        for s in range(UNITS + 5):
+            on(norm, s - 2)
+            on(rope, s - 5)
+            on(t_x, s)
+            on(t_h, s - 3)
+            on(q_x, s)
+            if s == 0:
+                tables_vector()
+            if s == 1:
+                weights_up()
+            on(mx1, s - 1)
+            if s == 2:
+                tables_scalar()
+            on(q_h, s - 3)
+            on(mx2, s - 4)
+            on(load, s + AHEAD)

@@ -24,10 +24,11 @@ TPB = S // P
 UNIT = 2
 UPB = TPB // UNIT
 UNITS = B * UPB
-AHEAD = 5
+AHEAD = 6
 MANUAL = True
-VEC_COPY = (1, 3)
-VEC_MOD = 5
+VEC_MOD = 4
+VEC_COPY = (1,)
+LAG_M1, LAG_NORM, LAG_TH, LAG_CH, LAG_M2, LAG_ROPE = 3, 4, 5, 6, 7, 8
 
 FLOPS = 2 * B * S * (D * Q_RANK + Q_RANK * NOUT)
 
@@ -60,57 +61,60 @@ def tile_multiheadlatentattention_pa_t_kernel(tc, x, w_dq, q_a_norm, w_uq, out):
         w_raw = setup.tile([P, 4, 2 * Q_RANK], BF16)
         w_view = w_dq.rearrange("(a p e) c -> p a (e c)", a=4, p=P, e=2)
         nc.sync.dma_start(out=w_raw[:, 0:2, :], in_=w_view[:, 0:2, :])
-        load(0)
         nc.sync.dma_start(out=w_raw[:, 2:4, :], in_=w_view[:, 2:4, :])
-        for u in range(1, AHEAD):
+        for u in range(AHEAD):
             load(u)
         u_raw = setup.tile([P, 4, NOUT], BF16)
         nc.scalar.dma_start(out=u_raw[:], in_=w_uq.rearrange("(j p) n -> p j n", p=P))
-        g_b = const.tile([P, Q_RANK], BF16)
-        nc.gpsimd.dma_start(out=g_b[:], in_=q_a_norm.partition_broadcast(P))
 
-        ident_f = const.tile([P, P], F32)
-        make_identity(nc, ident_f[:])
         pos_i = setup.tile([P, TPB], I32)
         nc.gpsimd.iota(pos_i[:], pattern=[[1, TPB]], base=0, channel_multiplier=TPB)
+        ident_f = const.tile([P, P], F32)
+        make_identity(nc, ident_f[:])
+        g_b = const.tile([P, Q_RANK], BF16)
+        nc.gpsimd.dma_start(out=g_b[:], in_=q_a_norm.partition_broadcast(P))
         ident_b = const.tile([P, P], BF16)
         make_identity(nc, ident_b[:])
 
+        zero = setup.tile([P, 1], F32)
+        nc.vector.memset(zero[:], 0.0)
+        warm = setup.tile([P, 1], F32)
+        nc.scalar.activation(out=warm[:], in_=zero[:], func=ACT.Sin)
         pos_f = setup.tile([P, TPB], F32)
         nc.vector.tensor_copy(out=pos_f[:], in_=pos_i[:])
-        turn_i = setup.tile([P, 2, TPB, HALF], I32)
-        turn_lo = setup.tile([P, TPB, HALF], F32)
+        turn_i = setup.tile([P, 2, HALF, TPB], I32)
+        turn_lo = setup.tile([P, HALF, TPB], F32)
         for i in range(HALF):
             freq = 1.0 / THETA ** (i / HALF) / (2.0 * math.pi)
             f_hi = math.floor(freq * GRID)
             f_lo = freq - f_hi / GRID
-            nc.vector.tensor_scalar(out=turn_i[:, 0, :, i], in0=pos_f[:], scalar1=float(f_hi),
+            nc.vector.tensor_scalar(out=turn_i[:, 0, i, :], in0=pos_f[:], scalar1=float(f_hi),
                                     scalar2=float(GRID // 2), op0=ALU.mult, op1=ALU.add)
-            nc.vector.tensor_scalar(out=turn_lo[:, :, i], in0=pos_f[:], scalar1=f_lo,
-                                    scalar2=None, op0=ALU.mult)
+            nc.scalar.activation(out=turn_lo[:, i, :], in_=pos_f[:], func=ACT.Copy, scale=f_lo)
+        nc.vector.tensor_scalar(out=turn_i[:, 1], in0=turn_i[:, 0], scalar1=float(GRID // 4),
+                                scalar2=None, op0=ALU.add)
+        nc.vector.tensor_scalar(out=turn_i[:], in0=turn_i[:], scalar1=GRID - 1,
+                                scalar2=None, op0=ALU.bitwise_and)
         frac = setup.tile([P, 2, TPB * HALF], F32)
-        negf = setup.tile([P, 2, TPB, HALF], F32)
+        negf = setup.tile([P, 2, HALF, TPB], F32)
         cos_t = const.tile([P, TPB, HALF], F32)
         sin_t = const.tile([P, TPB, 2, HALF], F32)
 
         def tables_vector():
-            nc.vector.tensor_scalar(out=turn_i[:, 1], in0=turn_i[:, 0], scalar1=float(GRID // 4),
-                                    scalar2=None, op0=ALU.add)
-            nc.vector.tensor_scalar(out=turn_i[:], in0=turn_i[:], scalar1=GRID - 1,
-                                    scalar2=None, op0=ALU.bitwise_and)
             nc.vector.scalar_tensor_tensor(
-                out=frac[:], in0=turn_i[:].rearrange("p a t i -> p a (t i)"), scalar=1.0 / GRID,
-                in1=turn_lo[:].rearrange("p t i -> p (t i)").unsqueeze(1).to_broadcast([P, 2, TPB * HALF]),
+                out=frac[:], in0=turn_i[:].rearrange("p a i t -> p a (i t)"), scalar=1.0 / GRID,
+                in1=turn_lo[:].rearrange("p i t -> p (i t)").unsqueeze(1).to_broadcast([P, 2, TPB * HALF]),
                 op0=ALU.mult, op1=ALU.add)
             nc.vector.scalar_tensor_tensor(
-                out=negf[:].rearrange("p a t i -> p a (t i)"), in0=frac[:], scalar=1.0, in1=frac[:],
+                out=negf[:].rearrange("p a i t -> p a (i t)"), in0=frac[:], scalar=1.0, in1=frac[:],
                 op0=ALU.is_ge, op1=ALU.subtract)
 
         def tables_scalar():
-            nc.scalar.activation(out=cos_t[:], in_=negf[:, 1], func=ACT.Sin, scale=-2.0 * math.pi, bias=-math.pi)
-            nc.scalar.activation(out=sin_t[:, :, 0, :], in_=negf[:, 0], func=ACT.Sin,
+            by_pos = negf[:].rearrange("p a i t -> p a t i")
+            nc.scalar.activation(out=cos_t[:], in_=by_pos[:, 1], func=ACT.Sin, scale=-2.0 * math.pi, bias=-math.pi)
+            nc.scalar.activation(out=sin_t[:, :, 0, :], in_=by_pos[:, 0], func=ACT.Sin,
                                  scale=-2.0 * math.pi, bias=-math.pi)
-            nc.scalar.activation(out=sin_t[:, :, 1, :], in_=negf[:, 0], func=ACT.Sin,
+            nc.scalar.activation(out=sin_t[:, :, 1, :], in_=by_pos[:, 0], func=ACT.Sin,
                                  scale=2.0 * math.pi, bias=math.pi)
 
         wdq_c = const.tile([P, 2, Q_RANK], U32, align_bytes=64)
@@ -136,74 +140,77 @@ def tile_multiheadlatentattention_pa_t_kernel(tc, x, w_dq, q_a_norm, w_uq, out):
             nc.vector.quantize_mx(out=wuq_c[:].bitcast(FP8X4), scales=wuq_s[:],
                                   in_=u_grp[:].rearrange("p r h f j -> p (r h f j)"))
 
-        def t_x(u):
-            x_sb = st["x", u]
-            xg = work.tile([P, UNIT, 2, P, 4], BF16, align_bytes=64, name="xg")
-            for i in range(UNIT):
-                xt = psum.tile([P, 4, P], F32, name="xt", bufs=2)
-                words = x_sb[:, i, :].bitcast(F32)
-                for a in range(4):
-                    nc.tensor.transpose(xt[:, a, :], words[:, a * P:(a + 1) * P], ident_f[:])
-                planes = xt[:].rearrange("p (g u) w -> p g w u", u=2)
-                if i == 1 and u % VEC_MOD in VEC_COPY:
-                    nc.vector.tensor_copy(out=xg[:, i].bitcast(F32), in_=planes)
-                else:
-                    nc.scalar.copy(out=xg[:, i].bitcast(F32), in_=planes)
-            st["xg", u] = xg
+        def t_x(u, i):
+            if i == 0:
+                st["xg", u] = work.tile([P, UNIT, 2, P, 4], BF16, align_bytes=64, name="xg")
+            xt = psum.tile([P, 4, P], F32, name="xt", bufs=2)
+            words = st["x", u][:, i, :].bitcast(F32)
+            for a in range(4):
+                nc.tensor.transpose(xt[:, a, :], words[:, a * P:(a + 1) * P], ident_f[:])
+            st["xt", u, i] = xt
+
+        def c_x(u, i):
+            planes = st["xt", u, i][:].rearrange("p (g u) w -> p g w u", u=2)
+            dst = st["xg", u][:, i].bitcast(F32)
+            if i == 1 and u % VEC_MOD in VEC_COPY:
+                nc.vector.tensor_copy(out=dst, in_=planes)
+            else:
+                nc.scalar.copy(out=dst, in_=planes)
 
         def q_x(u):
-            xg = st["xg", u]
-            xc = work.tile([P, UNIT * 2 * P], U32, align_bytes=64, name="xc")
-            xs = work.tile([P, UNIT * 2 * P], U8, align_bytes=64, name="xs")
+            xc = work.tile([P, UNIT * 2 * P], U32, align_bytes=64, name="xc", bufs=5)
+            xs = work.tile([P, UNIT * 2 * P], U8, align_bytes=64, name="xs", bufs=5)
             nc.vector.quantize_mx(out=xc[:].bitcast(FP8X4), scales=xs[:],
-                                  in_=xg[:].rearrange("p i g w t -> p (i g w t)"))
+                                  in_=st["xg", u][:].rearrange("p i g w t -> p (i g w t)"))
             st["xc", u] = (xc, xs)
 
-        def mx1(u):
+        def mx1(u, i):
             xc, xs = st["xc", u]
-            ss = small.tile([P, UNIT], F32, name="ss")
-            cs = []
-            for i in range(UNIT):
-                c_ps = psum.tile([P, Q_RANK], F32, name="c_ps", bufs=4)
-                for g in range(2):
-                    cols = slice((2 * i + g) * P, (2 * i + g + 1) * P)
-                    nc.tensor.matmul_mx(out=c_ps[:], lhsT=xc[:, cols].bitcast(FP8X4), lhsT_scale=xs[:, cols],
-                                        rhs=wdq_c[:, g, :].bitcast(FP8X4), rhs_scale=wdq_s[:, g, :],
-                                        start=(g == 0), stop=(g == 1))
-                cs.append(c_ps)
-            for i in range(UNIT):
-                junk = work.tile([P, Q_RANK], BF16, name="junk")
-                nc.scalar.activation(out=junk[:], in_=cs[i][:], func=ACT.Square, accum_out=ss[:, i:i + 1])
+            c_ps = psum.tile([P, Q_RANK], F32, name="c_ps", bufs=3)
+            for g in range(2):
+                cols = slice((2 * i + g) * P, (2 * i + g + 1) * P)
+                nc.tensor.matmul_mx(out=c_ps[:], lhsT=xc[:, cols].bitcast(FP8X4), lhsT_scale=xs[:, cols],
+                                    rhs=wdq_c[:, g, :].bitcast(FP8X4), rhs_scale=wdq_s[:, g, :],
+                                    start=(g == 0), stop=(g == 1))
+            st["c", u, i] = c_ps
+
+        def s_q(u, i):
+            if i == 0:
+                st["ss", u] = small.tile([P, UNIT], F32, name="ss")
+            junk = work.tile([P, Q_RANK], BF16, name="junk")
+            nc.scalar.activation(out=junk[:], in_=st["c", u, i][:], func=ACT.Square,
+                                 accum_out=st["ss", u][:, i:i + 1])
+
+        def r_t(u):
             rms = small.tile([P, UNIT], F32, name="rms")
-            nc.scalar.activation(out=rms[:], in_=ss[:], func=ACT.Sqrt, scale=1.0 / Q_RANK, bias=EPS)
-            st["c", u] = (cs, rms)
+            nc.scalar.activation(out=rms[:], in_=st["ss", u][:], func=ACT.Sqrt, scale=1.0 / Q_RANK, bias=EPS)
+            st["rms", u] = rms
 
         def norm(u):
-            cs, rms = st["c", u]
             rstd = small.tile([P, UNIT], F32, name="rstd")
-            nc.vector.reciprocal(rstd[:], rms[:])
+            nc.vector.reciprocal(rstd[:], st["rms", u][:])
             h_sb = work.tile([P, UNIT, Q_RANK], BF16, name="h_sb")
             for i in range(UNIT):
-                nc.vector.scalar_tensor_tensor(out=h_sb[:, i, :], in0=cs[i][:], scalar=rstd[:, i:i + 1],
+                nc.vector.scalar_tensor_tensor(out=h_sb[:, i, :], in0=st["c", u, i][:], scalar=rstd[:, i:i + 1],
                                                in1=g_b[:], op0=ALU.mult, op1=ALU.mult)
             st["h", u] = h_sb
 
-        def t_h(u):
-            h_sb = st["h", u]
-            ht = psum.tile([P, UNIT, 4, P], BF16, name="ht", bufs=1)
-            for i in range(UNIT):
-                for j in range(4):
-                    nc.tensor.transpose(ht[:, i, j, :], h_sb[:, i, j * P:(j + 1) * P], ident_b[:])
+        def t_h(u, i):
+            if i == 0:
+                st["ht", u] = psum.tile([P, UNIT, 4, P], BF16, name="ht", bufs=2)
+            for j in range(4):
+                nc.tensor.transpose(st["ht", u][:, i, j, :], st["h", u][:, i, j * P:(j + 1) * P], ident_b[:])
+
+        def c_h(u):
             hg = work.tile([P, UNIT, P, 4], BF16, align_bytes=64, name="hg")
-            nc.scalar.copy(out=hg[:], in_=ht[:].rearrange("p i j w -> p i w j"))
+            nc.scalar.copy(out=hg[:], in_=st["ht", u][:].rearrange("p i j w -> p i w j"))
             st["hg", u] = hg
 
         def q_h(u):
-            hg = st["hg", u]
             hc = work.tile([P, UNIT * P], U32, align_bytes=64, name="hc")
             hs = work.tile([P, UNIT * P], U8, align_bytes=64, name="hs")
             nc.vector.quantize_mx(out=hc[:].bitcast(FP8X4), scales=hs[:],
-                                  in_=hg[:].rearrange("p i w j -> p (i w j)"))
+                                  in_=st["hg", u][:].rearrange("p i w j -> p (i w j)"))
             st["hc", u] = (hc, hs)
 
         def mx2(u):
@@ -239,23 +246,32 @@ def tile_multiheadlatentattention_pa_t_kernel(tc, x, w_dq, q_a_norm, w_uq, out):
                                         in0=by_cos[:, :, :, r, :], in1=by_sin[:, :, :, 1 - r, :], op=ALU.add)
             nc.sync.dma_start(out=ov[b, :, t0:t0 + UNIT, :], in_=o_sb[:].rearrange("p i h f -> p i (h f)"))
 
-        def on(fn, u):
+        def on(fn, u, *half):
             if 0 <= u < UNITS:
-                fn(u)
+                fn(u, *half)
 
-        for s in range(UNITS + 5):
-            on(norm, s - 2)
-            on(rope, s - 5)
-            on(t_x, s)
-            on(t_h, s - 3)
-            on(q_x, s)
-            if s == 0:
-                tables_vector()
-            if s == 1:
-                weights_up()
-            on(mx1, s - 1)
-            if s == 2:
+        for s in range(UNITS + LAG_ROPE):
+            on(rope, s - LAG_ROPE)
+            on(norm, s - LAG_NORM)
+            on(t_x, s, 0)
+            on(c_x, s, 0)
+            on(t_h, s - LAG_TH, 0)
+            on(mx1, s - LAG_M1, 0)
+            on(c_h, s - LAG_CH)
+            on(s_q, s - LAG_M1, 0)
+            on(t_x, s, 1)
+            on(t_h, s - LAG_TH, 1)
+            on(mx1, s - LAG_M1, 1)
+            on(mx2, s - LAG_M2)
+            on(c_x, s, 1)
+            on(s_q, s - LAG_M1, 1)
+            if s == LAG_M1:
                 tables_scalar()
-            on(q_h, s - 3)
-            on(mx2, s - 4)
+            on(r_t, s - LAG_M1)
+            on(q_x, s - 1)
+            if s == 1:
+                tables_vector()
+            if s == 2:
+                weights_up()
+            on(q_h, s - LAG_CH)
             on(load, s + AHEAD)

@@ -27,8 +27,8 @@ UNITS = B * UPB
 AHEAD = 6
 MANUAL = True
 VEC_MOD = 4
-VEC_COPY = (1,)
-LAG_M1, LAG_NORM, LAG_TH, LAG_CH, LAG_M2, LAG_ROPE = 3, 4, 5, 6, 7, 8
+VEC_COPY = (3,)
+LAG_M1, LAG_NORM, LAG_TH, LAG_CH, LAG_QH, LAG_M2, LAG_ROPE = 3, 4, 5, 5, 6, 7, 8
 
 FLOPS = 2 * B * S * (D * Q_RANK + Q_RANK * NOUT)
 
@@ -166,7 +166,7 @@ def tile_multiheadlatentattention_pa_t_kernel(tc, x, w_dq, q_a_norm, w_uq, out):
 
         def mx1(u, i):
             xc, xs = st["xc", u]
-            c_ps = psum.tile([P, Q_RANK], F32, name="c_ps", bufs=3)
+            c_ps = psum.tile([P, Q_RANK], F32, name="c_ps", bufs=4)
             for g in range(2):
                 cols = slice((2 * i + g) * P, (2 * i + g + 1) * P)
                 nc.tensor.matmul_mx(out=c_ps[:], lhsT=xc[:, cols].bitcast(FP8X4), lhsT_scale=xs[:, cols],
@@ -197,7 +197,7 @@ def tile_multiheadlatentattention_pa_t_kernel(tc, x, w_dq, q_a_norm, w_uq, out):
 
         def t_h(u, i):
             if i == 0:
-                st["ht", u] = psum.tile([P, UNIT, 4, P], BF16, name="ht", bufs=2)
+                st["ht", u] = psum.tile([P, UNIT, 4, P], BF16, name="ht", bufs=1)
             for j in range(4):
                 nc.tensor.transpose(st["ht", u][:, i, j, :], st["h", u][:, i, j * P:(j + 1) * P], ident_b[:])
 
@@ -253,25 +253,25 @@ def tile_multiheadlatentattention_pa_t_kernel(tc, x, w_dq, q_a_norm, w_uq, out):
         for s in range(UNITS + LAG_ROPE):
             on(rope, s - LAG_ROPE)
             on(norm, s - LAG_NORM)
+            on(mx1, s - LAG_M1, 0)
+            on(s_q, s - LAG_M1, 0)
             on(t_x, s, 0)
             on(c_x, s, 0)
             on(t_h, s - LAG_TH, 0)
-            on(mx1, s - LAG_M1, 0)
-            on(c_h, s - LAG_CH)
-            on(s_q, s - LAG_M1, 0)
-            on(t_x, s, 1)
             on(t_h, s - LAG_TH, 1)
+            on(c_h, s - LAG_CH)
             on(mx1, s - LAG_M1, 1)
-            on(mx2, s - LAG_M2)
-            on(c_x, s, 1)
             on(s_q, s - LAG_M1, 1)
             if s == LAG_M1:
                 tables_scalar()
             on(r_t, s - LAG_M1)
+            on(t_x, s, 1)
+            on(mx2, s - LAG_M2)
+            on(q_h, s - LAG_QH)
+            on(c_x, s, 1)
             on(q_x, s - 1)
             if s == 1:
                 tables_vector()
             if s == 2:
                 weights_up()
-            on(q_h, s - LAG_CH)
             on(load, s + AHEAD)

@@ -26,8 +26,8 @@ UPB = TPB // UNIT
 UNITS = B * UPB
 AHEAD = 6
 MANUAL = True
-VEC_MOD = 4
-VEC_COPY = (3,)
+VEC_MOD = 2
+VEC_COPY = (1,)
 LAG_M1, LAG_NORM, LAG_TH, LAG_CH, LAG_QH, LAG_M2, LAG_ROPE = 3, 4, 5, 5, 6, 7, 8
 
 FLOPS = 2 * B * S * (D * Q_RANK + Q_RANK * NOUT)
@@ -75,6 +75,8 @@ def tile_multiheadlatentattention_pa_t_kernel(tc, x, w_dq, q_a_norm, w_uq, out):
         nc.gpsimd.dma_start(out=g_b[:], in_=q_a_norm.partition_broadcast(P))
         ident_b = const.tile([P, P], BF16)
         make_identity(nc, ident_b[:])
+        neg_half = const.tile([P, UNIT], F32)
+        nc.gpsimd.memset(neg_half[:], -0.5)
 
         zero = setup.tile([P, 1], F32)
         nc.vector.memset(zero[:], 0.0)
@@ -152,7 +154,7 @@ def tile_multiheadlatentattention_pa_t_kernel(tc, x, w_dq, q_a_norm, w_uq, out):
         def c_x(u, i):
             planes = st["xt", u, i][:].rearrange("p (g u) w -> p g w u", u=2)
             dst = st["xg", u][:, i].bitcast(F32)
-            if i == 1 and u % VEC_MOD in VEC_COPY:
+            if i == 1 and u % VEC_MOD in VEC_COPY and u < UNITS - 1:
                 nc.vector.tensor_copy(out=dst, in_=planes)
             else:
                 nc.scalar.copy(out=dst, in_=planes)
@@ -182,13 +184,15 @@ def tile_multiheadlatentattention_pa_t_kernel(tc, x, w_dq, q_a_norm, w_uq, out):
                                  accum_out=st["ss", u][:, i:i + 1])
 
         def r_t(u):
-            rms = small.tile([P, UNIT], F32, name="rms")
-            nc.scalar.activation(out=rms[:], in_=st["ss", u][:], func=ACT.Sqrt, scale=1.0 / Q_RANK, bias=EPS)
-            st["rms", u] = rms
+            ms = small.tile([P, UNIT], F32, name="ms")
+            nc.gpsimd.tensor_scalar(out=ms[:], in0=st["ss", u][:], scalar1=1.0 / Q_RANK, scalar2=EPS,
+                                    op0=ALU.mult, op1=ALU.add)
+            rstd = small.tile([P, UNIT], F32, name="rstd")
+            nc.gpsimd.tensor_tensor(out=rstd[:], in0=ms[:], in1=neg_half[:], op=ALU.pow)
+            st["rstd", u] = rstd
 
         def norm(u):
-            rstd = small.tile([P, UNIT], F32, name="rstd")
-            nc.vector.reciprocal(rstd[:], st["rms", u][:])
+            rstd = st["rstd", u]
             h_sb = work.tile([P, UNIT, Q_RANK], BF16, name="h_sb")
             for i in range(UNIT):
                 nc.vector.scalar_tensor_tensor(out=h_sb[:, i, :], in0=st["c", u, i][:], scalar=rstd[:, i:i + 1],
@@ -252,6 +256,7 @@ def tile_multiheadlatentattention_pa_t_kernel(tc, x, w_dq, q_a_norm, w_uq, out):
 
         for s in range(UNITS + LAG_ROPE):
             on(rope, s - LAG_ROPE)
+            on(q_h, s - LAG_QH)
             on(norm, s - LAG_NORM)
             on(mx1, s - LAG_M1, 0)
             on(s_q, s - LAG_M1, 0)
@@ -267,7 +272,6 @@ def tile_multiheadlatentattention_pa_t_kernel(tc, x, w_dq, q_a_norm, w_uq, out):
             on(r_t, s - LAG_M1)
             on(t_x, s, 1)
             on(mx2, s - LAG_M2)
-            on(q_h, s - LAG_QH)
             on(c_x, s, 1)
             on(q_x, s - 1)
             if s == 1:

@@ -27,7 +27,7 @@ UNITS = B * UPB
 AHEAD = 6
 MANUAL = True
 VEC_MOD = 2
-VEC_COPY = (1,)
+VEC_COPY = ()
 LAG_M1, LAG_NORM, LAG_TH, LAG_CH, LAG_QH, LAG_M2, LAG_ROPE = 3, 4, 5, 5, 6, 7, 8
 
 FLOPS = 2 * B * S * (D * Q_RANK + Q_RANK * NOUT)
@@ -256,7 +256,6 @@ def tile_multiheadlatentattention_pa_t_kernel(tc, x, w_dq, q_a_norm, w_uq, out):
 
         for s in range(UNITS + LAG_ROPE):
             on(rope, s - LAG_ROPE)
-            on(q_h, s - LAG_QH)
             on(norm, s - LAG_NORM)
             on(mx1, s - LAG_M1, 0)
             on(s_q, s - LAG_M1, 0)
@@ -272,6 +271,7 @@ def tile_multiheadlatentattention_pa_t_kernel(tc, x, w_dq, q_a_norm, w_uq, out):
             on(r_t, s - LAG_M1)
             on(t_x, s, 1)
             on(mx2, s - LAG_M2)
+            on(q_h, s - LAG_QH)
             on(c_x, s, 1)
             on(q_x, s - 1)
             if s == 1:

@@ -99,7 +99,8 @@ def tile_multiheadlatentattention_pa_t_kernel(tc, x, w_dq, q_a_norm, w_uq, out):
                                 scalar2=None, op0=ALU.bitwise_and)
         frac = setup.tile([P, 2, TPB * HALF], F32)
         negf = setup.tile([P, 2, HALF, TPB], F32)
-        cos_t = const.tile([P, TPB, HALF], F32)
+        cos_t = const.tile([P, TPB, QK], F32)
+        nc.gpsimd.memset(cos_t[:, :, 0:NOPE], 1.0)
         sin_t = const.tile([P, TPB, 2, HALF], F32)
 
         def tables_vector():
@@ -113,7 +114,9 @@ def tile_multiheadlatentattention_pa_t_kernel(tc, x, w_dq, q_a_norm, w_uq, out):
 
         def tables_scalar():
             by_pos = negf[:].rearrange("p a i t -> p a t i")
-            nc.scalar.activation(out=cos_t[:], in_=by_pos[:, 1], func=ACT.Sin, scale=-2.0 * math.pi, bias=-math.pi)
+            nc.scalar.activation(out=cos_t[:, :, NOPE:].rearrange("p t (r f) -> p t r f", r=2),
+                                 in_=by_pos[:, 1].unsqueeze(2).to_broadcast([P, TPB, 2, HALF]),
+                                 func=ACT.Sin, scale=-2.0 * math.pi, bias=-math.pi)
             nc.scalar.activation(out=sin_t[:, :, 0, :], in_=by_pos[:, 0], func=ACT.Sin,
                                  scale=-2.0 * math.pi, bias=-math.pi)
             nc.scalar.activation(out=sin_t[:, :, 1, :], in_=by_pos[:, 0], func=ACT.Sin,
@@ -133,14 +136,13 @@ def tile_multiheadlatentattention_pa_t_kernel(tc, x, w_dq, q_a_norm, w_uq, out):
                                   in_=w_grps[g][:].rearrange("p c t -> p (c t)"))
         wuq_c = const.tile([P, NOUT], U32, align_bytes=64)
         wuq_s = const.tile([P, NOUT], U8, align_bytes=64)
-        u_grp = setup.tile([P, 2, H, NOPE, 4], BF16, align_bytes=64)
+        u_grp = setup.tile([P, NOUT, 4], BF16, align_bytes=64)
 
         def weights_up():
-            u_src = u_raw[:].rearrange("p j (h r f) -> p r h f j", h=H, r=2)
-            for r in range(2):
-                nc.vector.tensor_copy(out=u_grp[:, r], in_=u_src[:, r])
+            nc.vector.tensor_copy(out=u_grp[:].rearrange("p (c i) t -> p c t i", i=4),
+                                  in_=u_raw[:].rearrange("p t (c i) -> p c t i", i=4))
             nc.vector.quantize_mx(out=wuq_c[:].bitcast(FP8X4), scales=wuq_s[:],
-                                  in_=u_grp[:].rearrange("p r h f j -> p (r h f j)"))
+                                  in_=u_grp[:].rearrange("p c t -> p (c t)"))
 
         def t_x(u, i):
             if i == 0:
@@ -230,24 +232,20 @@ def tile_multiheadlatentattention_pa_t_kernel(tc, x, w_dq, q_a_norm, w_uq, out):
             q_ps = st["q", u]
             b, t0 = u // UPB, (u % UPB) * UNIT
             o_sb = work.tile([P, UNIT, H, QK], F32, name="o_sb", bufs=4)
-            by_cos = work.tile([P, UNIT, H, 2, HALF], F32, name="by_cos")
-            by_sin = work.tile([P, UNIT, H, 2, HALF], F32, name="by_sin")
+            by_sin = work.tile([P, UNIT, H, ROPE], F32, name="by_sin")
+            heads = q_ps[:].rearrange("p i (h f) -> p i h f", h=H)
             nc.vector.tensor_tensor(
-                out=by_cos[:].rearrange("p i h r f -> p i (h r) f"),
-                in0=q_ps[:, :, H * NOPE:].rearrange("p i (a f) -> p i a f", f=HALF),
-                in1=cos_t[:, t0:t0 + UNIT, :].unsqueeze(2).to_broadcast([P, UNIT, 2 * H, HALF]),
-                op=ALU.mult)
-            nc.vector.tensor_tensor(
-                out=by_sin[:].rearrange("p i h r f -> p i h (r f)"),
-                in0=q_ps[:, :, H * NOPE:].rearrange("p i (h f) -> p i h f", h=H),
+                out=by_sin[:], in0=heads[:, :, :, NOPE:],
                 in1=sin_t[:, t0:t0 + UNIT].rearrange("p i r f -> p i (r f)").unsqueeze(2).to_broadcast(
                     [P, UNIT, H, ROPE]),
                 op=ALU.mult)
-            nc.vector.tensor_copy(out=o_sb[:, :, :, 0:NOPE],
-                                  in_=q_ps[:, :, 0:H * NOPE].rearrange("p i (h f) -> p i h f", h=H))
+            nc.vector.tensor_tensor(
+                out=o_sb[:], in0=heads,
+                in1=cos_t[:, t0:t0 + UNIT, :].unsqueeze(2).to_broadcast([P, UNIT, H, QK]), op=ALU.mult)
             for r in range(2):
-                nc.gpsimd.tensor_tensor(out=o_sb[:, :, :, NOPE + r * HALF:NOPE + (r + 1) * HALF],
-                                        in0=by_cos[:, :, :, r, :], in1=by_sin[:, :, :, 1 - r, :], op=ALU.add)
+                half = o_sb[:, :, :, NOPE + r * HALF:NOPE + (r + 1) * HALF]
+                nc.gpsimd.tensor_tensor(out=half, in0=half, in1=by_sin[:, :, :, (1 - r) * HALF:(2 - r) * HALF],
+                                        op=ALU.add)
             nc.sync.dma_start(out=ov[b, :, t0:t0 + UNIT, :], in_=o_sb[:].rearrange("p i h f -> p i (h f)"))
 
         def on(fn, u, *half):

@@ -75,8 +75,6 @@ def tile_multiheadlatentattention_pa_t_kernel(tc, x, w_dq, q_a_norm, w_uq, out):
         nc.gpsimd.dma_start(out=g_b[:], in_=q_a_norm.partition_broadcast(P))
         ident_b = const.tile([P, P], BF16)
         make_identity(nc, ident_b[:])
-        neg_half = const.tile([P, UNIT], F32)
-        nc.gpsimd.memset(neg_half[:], -0.5)
 
         zero = setup.tile([P, 1], F32)
         nc.vector.memset(zero[:], 0.0)
@@ -99,8 +97,7 @@ def tile_multiheadlatentattention_pa_t_kernel(tc, x, w_dq, q_a_norm, w_uq, out):
                                 scalar2=None, op0=ALU.bitwise_and)
         frac = setup.tile([P, 2, TPB * HALF], F32)
         negf = setup.tile([P, 2, HALF, TPB], F32)
-        cos_t = const.tile([P, TPB, QK], F32)
-        nc.gpsimd.memset(cos_t[:, :, 0:NOPE], 1.0)
+        cos_t = const.tile([P, TPB, HALF], F32)
         sin_t = const.tile([P, TPB, 2, HALF], F32)
 
         def tables_vector():
@@ -114,9 +111,7 @@ def tile_multiheadlatentattention_pa_t_kernel(tc, x, w_dq, q_a_norm, w_uq, out):
 
         def tables_scalar():
             by_pos = negf[:].rearrange("p a i t -> p a t i")
-            nc.scalar.activation(out=cos_t[:, :, NOPE:].rearrange("p t (r f) -> p t r f", r=2),
-                                 in_=by_pos[:, 1].unsqueeze(2).to_broadcast([P, TPB, 2, HALF]),
-                                 func=ACT.Sin, scale=-2.0 * math.pi, bias=-math.pi)
+            nc.scalar.activation(out=cos_t[:], in_=by_pos[:, 1], func=ACT.Sin, scale=-2.0 * math.pi, bias=-math.pi)
             nc.scalar.activation(out=sin_t[:, :, 0, :], in_=by_pos[:, 0], func=ACT.Sin,
                                  scale=-2.0 * math.pi, bias=-math.pi)
             nc.scalar.activation(out=sin_t[:, :, 1, :], in_=by_pos[:, 0], func=ACT.Sin,
@@ -136,13 +131,14 @@ def tile_multiheadlatentattention_pa_t_kernel(tc, x, w_dq, q_a_norm, w_uq, out):
                                   in_=w_grps[g][:].rearrange("p c t -> p (c t)"))
         wuq_c = const.tile([P, NOUT], U32, align_bytes=64)
         wuq_s = const.tile([P, NOUT], U8, align_bytes=64)
-        u_grp = setup.tile([P, NOUT, 4], BF16, align_bytes=64)
+        u_grp = setup.tile([P, 2, H, NOPE, 4], BF16, align_bytes=64)
 
         def weights_up():
-            nc.vector.tensor_copy(out=u_grp[:].rearrange("p (c i) t -> p c t i", i=4),
-                                  in_=u_raw[:].rearrange("p t (c i) -> p c t i", i=4))
+            u_src = u_raw[:].rearrange("p j (h r f) -> p r h f j", h=H, r=2)
+            for r in range(2):
+                nc.vector.tensor_copy(out=u_grp[:, r], in_=u_src[:, r])
             nc.vector.quantize_mx(out=wuq_c[:].bitcast(FP8X4), scales=wuq_s[:],
-                                  in_=u_grp[:].rearrange("p c t -> p (c t)"))
+                                  in_=u_grp[:].rearrange("p r h f j -> p (r h f j)"))
 
         def t_x(u, i):
             if i == 0:
@@ -186,11 +182,9 @@ def tile_multiheadlatentattention_pa_t_kernel(tc, x, w_dq, q_a_norm, w_uq, out):
                                  accum_out=st["ss", u][:, i:i + 1])
 
         def r_t(u):
-            ms = small.tile([P, UNIT], F32, name="ms")
-            nc.gpsimd.tensor_scalar(out=ms[:], in0=st["ss", u][:], scalar1=1.0 / Q_RANK, scalar2=EPS,
-                                    op0=ALU.mult, op1=ALU.add)
             rstd = small.tile([P, UNIT], F32, name="rstd")
-            nc.gpsimd.tensor_tensor(out=rstd[:], in0=ms[:], in1=neg_half[:], op=ALU.pow)
+            nc.scalar.activation(out=rstd[:], in_=st["ss", u][:], func=ACT.Abs_reciprocal_sqrt,
+                                 scale=1.0 / Q_RANK, bias=EPS)
             st["rstd", u] = rstd
 
         def norm(u):
@@ -232,20 +226,24 @@ def tile_multiheadlatentattention_pa_t_kernel(tc, x, w_dq, q_a_norm, w_uq, out):
             q_ps = st["q", u]
             b, t0 = u // UPB, (u % UPB) * UNIT
             o_sb = work.tile([P, UNIT, H, QK], F32, name="o_sb", bufs=4)
-            by_sin = work.tile([P, UNIT, H, ROPE], F32, name="by_sin")
-            heads = q_ps[:].rearrange("p i (h f) -> p i h f", h=H)
+            by_cos = work.tile([P, UNIT, H, 2, HALF], F32, name="by_cos")
+            by_sin = work.tile([P, UNIT, H, 2, HALF], F32, name="by_sin")
             nc.vector.tensor_tensor(
-                out=by_sin[:], in0=heads[:, :, :, NOPE:],
+                out=by_cos[:].rearrange("p i h r f -> p i (h r) f"),
+                in0=q_ps[:, :, H * NOPE:].rearrange("p i (a f) -> p i a f", f=HALF),
+                in1=cos_t[:, t0:t0 + UNIT, :].unsqueeze(2).to_broadcast([P, UNIT, 2 * H, HALF]),
+                op=ALU.mult)
+            nc.vector.tensor_tensor(
+                out=by_sin[:].rearrange("p i h r f -> p i h (r f)"),
+                in0=q_ps[:, :, H * NOPE:].rearrange("p i (h f) -> p i h f", h=H),
                 in1=sin_t[:, t0:t0 + UNIT].rearrange("p i r f -> p i (r f)").unsqueeze(2).to_broadcast(
                     [P, UNIT, H, ROPE]),
                 op=ALU.mult)
-            nc.vector.tensor_tensor(
-                out=o_sb[:], in0=heads,
-                in1=cos_t[:, t0:t0 + UNIT, :].unsqueeze(2).to_broadcast([P, UNIT, H, QK]), op=ALU.mult)
+            nc.vector.tensor_copy(out=o_sb[:, :, :, 0:NOPE],
+                                  in_=q_ps[:, :, 0:H * NOPE].rearrange("p i (h f) -> p i h f", h=H))
             for r in range(2):
-                half = o_sb[:, :, :, NOPE + r * HALF:NOPE + (r + 1) * HALF]
-                nc.gpsimd.tensor_tensor(out=half, in0=half, in1=by_sin[:, :, :, (1 - r) * HALF:(2 - r) * HALF],
-                                        op=ALU.add)
+                nc.gpsimd.tensor_tensor(out=o_sb[:, :, :, NOPE + r * HALF:NOPE + (r + 1) * HALF],
+                                        in0=by_cos[:, :, :, r, :], in1=by_sin[:, :, :, 1 - r, :], op=ALU.add)
             nc.sync.dma_start(out=ov[b, :, t0:t0 + UNIT, :], in_=o_sb[:].rearrange("p i h f -> p i (h f)"))
 
         def on(fn, u, *half):

@@ -28,7 +28,7 @@ AHEAD = 6
 MANUAL = True
 VEC_MOD = 2
 VEC_COPY = ()
-LAG_M1, LAG_NORM, LAG_TH, LAG_CH, LAG_QH, LAG_M2, LAG_ROPE = 3, 4, 5, 5, 6, 7, 8
+LAG_M1, LAG_NORM, LAG_TH, LAG_CH, LAG_QH, LAG_M2, LAG_ROPE = 3, 4, 5, 5, 5, 6, 7
 
 FLOPS = 2 * B * S * (D * Q_RANK + Q_RANK * NOUT)
 
@@ -75,6 +75,8 @@ def tile_multiheadlatentattention_pa_t_kernel(tc, x, w_dq, q_a_norm, w_uq, out):
         nc.gpsimd.dma_start(out=g_b[:], in_=q_a_norm.partition_broadcast(P))
         ident_b = const.tile([P, P], BF16)
         make_identity(nc, ident_b[:])
+        neg_half = const.tile([P, UNIT], F32)
+        nc.gpsimd.memset(neg_half[:], -0.5)
 
         zero = setup.tile([P, 1], F32)
         nc.vector.memset(zero[:], 0.0)
@@ -114,8 +116,10 @@ def tile_multiheadlatentattention_pa_t_kernel(tc, x, w_dq, q_a_norm, w_uq, out):
             nc.scalar.activation(out=cos_t[:], in_=by_pos[:, 1], func=ACT.Sin, scale=-2.0 * math.pi, bias=-math.pi)
             nc.scalar.activation(out=sin_t[:, :, 0, :], in_=by_pos[:, 0], func=ACT.Sin,
                                  scale=-2.0 * math.pi, bias=-math.pi)
-            nc.scalar.activation(out=sin_t[:, :, 1, :], in_=by_pos[:, 0], func=ACT.Sin,
-                                 scale=2.0 * math.pi, bias=math.pi)
+
+        def tables_negate():
+            nc.gpsimd.tensor_scalar(out=sin_t[:, :, 1, :], in0=sin_t[:, :, 0, :], scalar1=-1.0, scalar2=0.0,
+                                    op0=ALU.mult, op1=ALU.add)
 
         wdq_c = const.tile([P, 2, Q_RANK], U32, align_bytes=64)
         wdq_s = const.tile([P, 2, Q_RANK], U8, align_bytes=64)
@@ -182,9 +186,11 @@ def tile_multiheadlatentattention_pa_t_kernel(tc, x, w_dq, q_a_norm, w_uq, out):
                                  accum_out=st["ss", u][:, i:i + 1])
 
         def r_t(u):
+            ms = small.tile([P, UNIT], F32, name="ms")
+            nc.gpsimd.tensor_scalar(out=ms[:], in0=st["ss", u][:], scalar1=1.0 / Q_RANK, scalar2=EPS,
+                                    op0=ALU.mult, op1=ALU.add)
             rstd = small.tile([P, UNIT], F32, name="rstd")
-            nc.scalar.activation(out=rstd[:], in_=st["ss", u][:], func=ACT.Abs_reciprocal_sqrt,
-                                 scale=1.0 / Q_RANK, bias=EPS)
+            nc.gpsimd.tensor_tensor(out=rstd[:], in0=ms[:], in1=neg_half[:], op=ALU.pow)
             st["rstd", u] = rstd
 
         def norm(u):
@@ -241,8 +247,9 @@ def tile_multiheadlatentattention_pa_t_kernel(tc, x, w_dq, q_a_norm, w_uq, out):
                 op=ALU.mult)
             nc.vector.tensor_copy(out=o_sb[:, :, :, 0:NOPE],
                                   in_=q_ps[:, :, 0:H * NOPE].rearrange("p i (h f) -> p i h f", h=H))
+            adder = nc.vector if u == UNITS - 1 else nc.gpsimd
             for r in range(2):
-                nc.gpsimd.tensor_tensor(out=o_sb[:, :, :, NOPE + r * HALF:NOPE + (r + 1) * HALF],
+                adder.tensor_tensor(out=o_sb[:, :, :, NOPE + r * HALF:NOPE + (r + 1) * HALF],
                                         in0=by_cos[:, :, :, r, :], in1=by_sin[:, :, :, 1 - r, :], op=ALU.add)
             nc.sync.dma_start(out=ov[b, :, t0:t0 + UNIT, :], in_=o_sb[:].rearrange("p i h f -> p i (h f)"))
 
@@ -265,13 +272,15 @@ def tile_multiheadlatentattention_pa_t_kernel(tc, x, w_dq, q_a_norm, w_uq, out):
             if s == LAG_M1:
                 tables_scalar()
             on(r_t, s - LAG_M1)
+            if s == LAG_M1:
+                tables_negate()
             on(t_x, s, 1)
             on(mx2, s - LAG_M2)
-            on(q_h, s - LAG_QH)
             on(c_x, s, 1)
             on(q_x, s - 1)
             if s == 1:
                 tables_vector()
             if s == 2:
                 weights_up()
+            on(q_h, s - LAG_QH)
             on(load, s + AHEAD)

from contextlib import ExitStack
import math

import concourse.mybir as mybir
from concourse.masks import make_identity

F32 = mybir.dt.float32
BF16 = mybir.dt.bfloat16
I32 = mybir.dt.int32
U32 = mybir.dt.uint32
U8 = mybir.dt.uint8
FP8X4 = mybir.dt.float8_e4m3fn_x4
ALU = mybir.AluOpType
ACT = mybir.ActivationFunctionType

P = 128
B, S, D, H, NOPE, ROPE, Q_RANK = 4, 2048, 1024, 2, 64, 64, 512
QK = NOPE + ROPE
HALF = ROPE // 2
NOUT = H * QK
EPS = 1e-6
THETA = 10000.0
TPB = S // P
UNIT = 2
UPB = TPB // UNIT
UNITS = B * UPB
AHEAD = 6
MANUAL = True
VEC_MOD = 2
VEC_COPY = ()
LAG_M1, LAG_NORM, LAG_TH, LAG_CH, LAG_QH, LAG_M2, LAG_ROPE = 3, 4, 5, 5, 5, 6, 7

FLOPS = 2 * B * S * (D * Q_RANK + Q_RANK * NOUT)

GRID = 2 ** 15


def tile_multiheadlatentattention_pa_t_kernel(tc, x, w_dq, q_a_norm, w_uq, out):
    nc = tc.nc
    xv = x.rearrange("b (p t) k -> b p t k", t=TPB)
    ov = out.rearrange("b (p t) h f -> b p t (h f)", t=TPB)

    with ExitStack() as ctx:
        const = ctx.enter_context(tc.tile_pool(name="const", bufs=1))
        setup = ctx.enter_context(tc.tile_pool(name="setup", bufs=1))
        xpool = ctx.enter_context(tc.tile_pool(name="xpool", bufs=AHEAD + 1))
        work = ctx.enter_context(tc.tile_pool(name="work", bufs=3))
        small = ctx.enter_context(tc.tile_pool(name="small", bufs=4))
        psum = ctx.enter_context(tc.psum_pool(name="psum", bufs=1))
        if MANUAL:
            ctx.enter_context(tc.manual_schedule())

        st = {}

        def load(u):
            x_sb = xpool.tile([P, UNIT, D], BF16, name="x_sb")
            b, t0 = u // UPB, (u % UPB) * UNIT
            nc.sync.dma_start(out=x_sb[:], in_=xv[b, :, t0:t0 + UNIT, :])
            st["x", u] = x_sb

        w_raw = setup.tile([P, 4, 2 * Q_RANK], BF16)
        w_view = w_dq.rearrange("(a p e) c -> p a (e c)", a=4, p=P, e=2)
        nc.sync.dma_start(out=w_raw[:, 0:2, :], in_=w_view[:, 0:2, :])
        nc.sync.dma_start(out=w_raw[:, 2:4, :], in_=w_view[:, 2:4, :])
        for u in range(AHEAD):
            load(u)
        u_raw = setup.tile([P, 4, NOUT], BF16)
        nc.scalar.dma_start(out=u_raw[:], in_=w_uq.rearrange("(j p) n -> p j n", p=P))

        pos_i = setup.tile([P, TPB], I32)
        nc.gpsimd.iota(pos_i[:], pattern=[[1, TPB]], base=0, channel_multiplier=TPB)
        ident_f = const.tile([P, P], F32)
        make_identity(nc, ident_f[:])
        g_b = const.tile([P, Q_RANK], BF16)
        nc.gpsimd.dma_start(out=g_b[:], in_=q_a_norm.partition_broadcast(P))
        ident_b = const.tile([P, P], BF16)
        make_identity(nc, ident_b[:])
        neg_half = const.tile([P, UNIT], F32)
        nc.gpsimd.memset(neg_half[:], -0.5)

        zero = setup.tile([P, 1], F32)
        nc.vector.memset(zero[:], 0.0)
        warm = setup.tile([P, 1], F32)
        nc.scalar.activation(out=warm[:], in_=zero[:], func=ACT.Sin)
        pos_f = setup.tile([P, TPB], F32)
        nc.vector.tensor_copy(out=pos_f[:], in_=pos_i[:])
        turn_i = setup.tile([P, 2, HALF, TPB], I32)
        turn_lo = setup.tile([P, HALF, TPB], F32)
        for i in range(HALF):
            freq = 1.0 / THETA ** (i / HALF) / (2.0 * math.pi)
            f_hi = math.floor(freq * GRID)
            f_lo = freq - f_hi / GRID
            nc.vector.tensor_scalar(out=turn_i[:, 0, i, :], in0=pos_f[:], scalar1=float(f_hi),
                                    scalar2=float(GRID // 2), op0=ALU.mult, op1=ALU.add)
            nc.scalar.activation(out=turn_lo[:, i, :], in_=pos_f[:], func=ACT.Copy, scale=f_lo)
        nc.vector.tensor_scalar(out=turn_i[:, 1], in0=turn_i[:, 0], scalar1=float(GRID // 4),
                                scalar2=None, op0=ALU.add)
        nc.vector.tensor_scalar(out=turn_i[:], in0=turn_i[:], scalar1=GRID - 1,
                                scalar2=None, op0=ALU.bitwise_and)
        frac = setup.tile([P, 2, TPB * HALF], F32)
        negf = setup.tile([P, 2, HALF, TPB], F32)
        cos_t = const.tile([P, TPB, HALF], F32)
        sin_t = const.tile([P, TPB, 2, HALF], F32)

        def tables_vector():
            nc.vector.scalar_tensor_tensor(
                out=frac[:], in0=turn_i[:].rearrange("p a i t -> p a (i t)"), scalar=1.0 / GRID,
                in1=turn_lo[:].rearrange("p i t -> p (i t)").unsqueeze(1).to_broadcast([P, 2, TPB * HALF]),
                op0=ALU.mult, op1=ALU.add)
            nc.vector.scalar_tensor_tensor(
                out=negf[:].rearrange("p a i t -> p a (i t)"), in0=frac[:], scalar=1.0, in1=frac[:],
                op0=ALU.is_ge, op1=ALU.subtract)

        def tables_scalar():
            by_pos = negf[:].rearrange("p a i t -> p a t i")
            nc.scalar.activation(out=cos_t[:], in_=by_pos[:, 1], func=ACT.Sin, scale=-2.0 * math.pi, bias=-math.pi)
            nc.scalar.activation(out=sin_t[:, :, 0, :], in_=by_pos[:, 0], func=ACT.Sin,
                                 scale=-2.0 * math.pi, bias=-math.pi)

        def tables_negate():
            nc.gpsimd.tensor_scalar(out=sin_t[:, :, 1, :], in0=sin_t[:, :, 0, :], scalar1=-1.0, scalar2=0.0,
                                    op0=ALU.mult, op1=ALU.add)

        wdq_c = const.tile([P, 2, Q_RANK], U32, align_bytes=64)
        wdq_s = const.tile([P, 2, Q_RANK], U8, align_bytes=64)
        w_grps = []
        for g in range(2):
            w_grp = setup.tile([P, Q_RANK, 4], BF16, align_bytes=64, name="w_grp%d" % g)
            w_src = w_raw[:, 2 * g:2 * g + 2, :].rearrange("p u (e c) -> p (u e) c", e=2)
            nc.vector.tensor_copy(out=w_grp[:].rearrange("p (c i) t -> p c t i", i=4),
                                  in_=w_src.rearrange("p t (c i) -> p c t i", i=4))
            w_grps.append(w_grp)
        for g in range(2):
            nc.vector.quantize_mx(out=wdq_c[:, g, :].bitcast(FP8X4), scales=wdq_s[:, g, :],
                                  in_=w_grps[g][:].rearrange("p c t -> p (c t)"))
        wuq_c = const.tile([P, NOUT], U32, align_bytes=64)
        wuq_s = const.tile([P, NOUT], U8, align_bytes=64)
        u_grp = setup.tile([P, 2, H, NOPE, 4], BF16, align_bytes=64)

        def weights_up():
            u_src = u_raw[:].rearrange("p j (h r f) -> p r h f j", h=H, r=2)
            for r in range(2):
                nc.vector.tensor_copy(out=u_grp[:, r], in_=u_src[:, r])
            nc.vector.quantize_mx(out=wuq_c[:].bitcast(FP8X4), scales=wuq_s[:],
                                  in_=u_grp[:].rearrange("p r h f j -> p (r h f j)"))

        def t_x(u, i):
            if i == 0:
                st["xg", u] = work.tile([P, UNIT, 2, P, 4], BF16, align_bytes=64, name="xg")
            xt = psum.tile([P, 4, P], F32, name="xt", bufs=2)
            words = st["x", u][:, i, :].bitcast(F32)
            for a in range(4):
                nc.tensor.transpose(xt[:, a, :], words[:, a * P:(a + 1) * P], ident_f[:])
            st["xt", u, i] = xt

        def c_x(u, i):
            planes = st["xt", u, i][:].rearrange("p (g u) w -> p g w u", u=2)
            dst = st["xg", u][:, i].bitcast(F32)
            if i == 1 and u % VEC_MOD in VEC_COPY and u < UNITS - 1:
                nc.vector.tensor_copy(out=dst, in_=planes)
            else:
                nc.scalar.copy(out=dst, in_=planes)

        def q_x(u):
            xc = work.tile([P, UNIT * 2 * P], U32, align_bytes=64, name="xc", bufs=5)
            xs = work.tile([P, UNIT * 2 * P], U8, align_bytes=64, name="xs", bufs=5)
            nc.vector.quantize_mx(out=xc[:].bitcast(FP8X4), scales=xs[:],
                                  in_=st["xg", u][:].rearrange("p i g w t -> p (i g w t)"))
            st["xc", u] = (xc, xs)

        def mx1(u, i):
            xc, xs = st["xc", u]
            c_ps = psum.tile([P, Q_RANK], F32, name="c_ps", bufs=4)
            for g in range(2):
                cols = slice((2 * i + g) * P, (2 * i + g + 1) * P)
                nc.tensor.matmul_mx(out=c_ps[:], lhsT=xc[:, cols].bitcast(FP8X4), lhsT_scale=xs[:, cols],
                                    rhs=wdq_c[:, g, :].bitcast(FP8X4), rhs_scale=wdq_s[:, g, :],
                                    start=(g == 0), stop=(g == 1))
            st["c", u, i] = c_ps

        def s_q(u, i):
            if i == 0:
                st["ss", u] = small.tile([P, UNIT], F32, name="ss")
            junk = work.tile([P, Q_RANK], BF16, name="junk")
            nc.scalar.activation(out=junk[:], in_=st["c", u, i][:], func=ACT.Square,
                                 accum_out=st["ss", u][:, i:i + 1])

        def r_t(u):
            ms = small.tile([P, UNIT], F32, name="ms")
            nc.gpsimd.tensor_scalar(out=ms[:], in0=st["ss", u][:], scalar1=1.0 / Q_RANK, scalar2=EPS,
                                    op0=ALU.mult, op1=ALU.add)
            rstd = small.tile([P, UNIT], F32, name="rstd")
            nc.gpsimd.tensor_tensor(out=rstd[:], in0=ms[:], in1=neg_half[:], op=ALU.pow)
            st["rstd", u] = rstd

        def norm(u):
            rstd = st["rstd", u]
            h_sb = work.tile([P, UNIT, Q_RANK], BF16, name="h_sb")
            for i in range(UNIT):
                nc.vector.scalar_tensor_tensor(out=h_sb[:, i, :], in0=st["c", u, i][:], scalar=rstd[:, i:i + 1],
                                               in1=g_b[:], op0=ALU.mult, op1=ALU.mult)
            st["h", u] = h_sb

        def t_h(u, i):
            if i == 0:
                st["ht", u] = psum.tile([P, UNIT, 4, P], BF16, name="ht", bufs=1)
            for j in range(4):
                nc.tensor.transpose(st["ht", u][:, i, j, :], st["h", u][:, i, j * P:(j + 1) * P], ident_b[:])

        def c_h(u):
            hg = work.tile([P, UNIT, P, 4], BF16, align_bytes=64, name="hg")
            nc.scalar.copy(out=hg[:], in_=st["ht", u][:].rearrange("p i j w -> p i w j"))
            st["hg", u] = hg

        def q_h(u):
            hc = work.tile([P, UNIT * P], U32, align_bytes=64, name="hc")
            hs = work.tile([P, UNIT * P], U8, align_bytes=64, name="hs")
            nc.vector.quantize_mx(out=hc[:].bitcast(FP8X4), scales=hs[:],
                                  in_=st["hg", u][:].rearrange("p i w j -> p (i w j)"))
            st["hc", u] = (hc, hs)

        def mx2(u):
            hc, hs = st["hc", u]
            q_ps = psum.tile([P, UNIT, NOUT], F32, name="q_ps", bufs=1)
            for i in range(UNIT):
                cols = slice(i * P, (i + 1) * P)
                nc.tensor.matmul_mx(out=q_ps[:, i, :], lhsT=hc[:, cols].bitcast(FP8X4), lhsT_scale=hs[:, cols],
                                    rhs=wuq_c[:].bitcast(FP8X4), rhs_scale=wuq_s[:], start=True, stop=True)
            st["q", u] = q_ps

        def rope(u):
            q_ps = st["q", u]
            b, t0 = u // UPB, (u % UPB) * UNIT
            o_sb = work.tile([P, UNIT, H, QK], F32, name="o_sb", bufs=4)
            by_cos = work.tile([P, UNIT, H, 2, HALF], F32, name="by_cos")
            by_sin = work.tile([P, UNIT, H, 2, HALF], F32, name="by_sin")
            nc.vector.tensor_tensor(
                out=by_cos[:].rearrange("p i h r f -> p i (h r) f"),
                in0=q_ps[:, :, H * NOPE:].rearrange("p i (a f) -> p i a f", f=HALF),
                in1=cos_t[:, t0:t0 + UNIT, :].unsqueeze(2).to_broadcast([P, UNIT, 2 * H, HALF]),
                op=ALU.mult)
            nc.vector.tensor_tensor(
                out=by_sin[:].rearrange("p i h r f -> p i h (r f)"),
                in0=q_ps[:, :, H * NOPE:].rearrange("p i (h f) -> p i h f", h=H),
                in1=sin_t[:, t0:t0 + UNIT].rearrange("p i r f -> p i (r f)").unsqueeze(2).to_broadcast(
                    [P, UNIT, H, ROPE]),
                op=ALU.mult)
            nc.vector.tensor_copy(out=o_sb[:, :, :, 0:NOPE],
                                  in_=q_ps[:, :, 0:H * NOPE].rearrange("p i (h f) -> p i h f", h=H))
            adder = nc.vector if u == UNITS - 1 else nc.gpsimd
            for r in range(2):
                adder.tensor_tensor(out=o_sb[:, :, :, NOPE + r * HALF:NOPE + (r + 1) * HALF],
                                        in0=by_cos[:, :, :, r, :], in1=by_sin[:, :, :, 1 - r, :], op=ALU.add)
            nc.sync.dma_start(out=ov[b, :, t0:t0 + UNIT, :], in_=o_sb[:].rearrange("p i h f -> p i (h f)"))

        def on(fn, u, *half):
            if 0 <= u < UNITS:
                fn(u, *half)

        for s in range(UNITS + LAG_ROPE):
            on(rope, s - LAG_ROPE)
            on(norm, s - LAG_NORM)
            on(mx1, s - LAG_M1, 0)
            on(s_q, s - LAG_M1, 0)
            on(t_x, s, 0)
            on(c_x, s, 0)
            on(t_h, s - LAG_TH, 0)
            on(t_h, s - LAG_TH, 1)
            on(c_h, s - LAG_CH)
            on(mx1, s - LAG_M1, 1)
            on(s_q, s - LAG_M1, 1)
            if s == LAG_M1:
                tables_scalar()
            on(r_t, s - LAG_M1)
            if s == LAG_M1:
                tables_negate()
            on(t_x, s, 1)
            on(mx2, s - LAG_M2)
            on(c_x, s, 1)
            on(q_x, s - 1)
            if s == 1:
                tables_vector()
            if s == 2:
                weights_up()
            on(q_h, s - LAG_QH)
            on(load, s + AHEAD)
